import numpy as np
import ml_dtypes

BF16 = ml_dtypes.bfloat16


def bf(x):
    return np.asarray(x, np.float32).astype(BF16)


def f32(x):
    return np.asarray(x, np.float32)


def f64(x):
    return np.asarray(x).astype(np.float64)


def striped(idx):
    return np.tile(idx.reshape(-1, 16).T, (8, 1))


C, S, E, R, P, N = 256, 2048, 512, 4, 2, 1024


def elu(v):
    return np.maximum(v, 0.0) + np.exp(np.minimum(v, 0.0)) - 1.0


def setup_inputs():
    return {"x": f32(0.6 * np.random.standard_normal((P, C, S))), "b0": f32(0.1 * np.random.standard_normal((C, 1))), "zp": f32(0.6 * np.random.standard_normal((C, R))), "w1": bf(np.random.standard_normal((C, C)) / np.sqrt(C)), "b1": f32(0.1 * np.random.standard_normal((C, 1))), "offs": striped(np.random.permutation(np.tile(np.arange(S), 2))[:N])}


def reference(x, b0, zp, w1, b1, offs):
    idx = offs[:16].T.reshape(-1)
    u = f64(x)[0][:, idx[:E]] + f64(b0)
    pair = f64(x)[1][:, idx[E:]] + u
    h = elu(pair[:, None, :] + f64(zp)[:, :, None]).reshape(C, R * E)
    return elu(f64(w1).T @ h + f64(b1))

@@ -1,0 +1,96 @@
+from contextlib import ExitStack
+
+import concourse.mybir as mybir
+
+F32 = mybir.dt.float32
+BF16 = mybir.dt.bfloat16
+U16 = mybir.dt.uint16
+ADD = mybir.AluOpType.add
+MIN = mybir.AluOpType.min
+MAX = mybir.AluOpType.max
+EXP = mybir.ActivationFunctionType.Exp
+
+P = 128
+C = 256
+S = 2048
+E = 512
+R = 4
+N = 2 * E
+BLOCKS = C // P
+PIECE = E // 16
+
+FLOPS = 2 * C * C * R * E
+
+
+def tile_bondgraphnetdecoder_kernel(tc, x, b0, zp, w1, b1, offs, out):
+    nc = tc.nc
+    with ExitStack() as ctx:
+        held = ctx.enter_context(tc.tile_pool(name="held", bufs=1))
+        psum = ctx.enter_context(tc.psum_pool(name="psum", bufs=1))
+
+        offsets = held.tile([P, N // 16], U16, name="offsets")
+        nc.sync.dma_start(offsets[:], offs)
+        window = {}
+        for k in range(BLOCKS):
+            for place in range(2):
+                window[place, k] = held.tile([P, S], F32, name=f"window{place}_{k}")
+                nc.sync.dma_start(window[place, k][:], x[place, k * P : (k + 1) * P, :])
+
+        b0_sb = held.tile([P, BLOCKS], F32, name="b0_sb")
+        zp_sb = held.tile([P, BLOCKS, R], F32, name="zp_sb")
+        b1_sb = held.tile([P, BLOCKS], F32, name="b1_sb")
+        w1_sb = held.tile([P, BLOCKS, C], BF16, name="w1_sb")
+        with nc.allow_non_contiguous_dma(reason="one to four floats per partition"):
+            nc.scalar.dma_start(b0_sb[:], b0.rearrange("(k p) o -> p (k o)", p=P))
+            nc.scalar.dma_start(zp_sb[:], zp.rearrange("(k p) r -> p k r", p=P))
+            nc.scalar.dma_start(b1_sb[:], b1.rearrange("(k p) o -> p (k o)", p=P))
+        nc.scalar.dma_start(w1_sb[:], w1.rearrange("(k p) m -> p k m", p=P))
+
+        zeros = held.tile([P, E], F32, name="zeros")
+        nc.vector.memset(zeros[:], 0.0)
+        b0_wide = {}
+        for k in range(BLOCKS):
+            b0_wide[k] = held.tile([P, E], F32, name=f"b0_wide{k}")
+            nc.vector.tensor_scalar_add(b0_wide[k][:], zeros[:], b0_sb[:, k : k + 1])
+
+        acc = {}
+        for m in range(BLOCKS):
+            for r in range(R):
+                acc[m, r] = psum.tile([P, E], F32, name=f"acc{m}_{r}")
+
+        for k in range(BLOCKS):
+            u = held.tile([P, E], F32, name=f"u{k}")
+            nc.vector.tensor_tensor(
+                u[:], window[0, k][:].indirect(offsets[:, 0:PIECE]), b0_wide[k][:], ADD
+            )
+            pair = held.tile([P, E], F32, name=f"pair{k}")
+            nc.vector.tensor_tensor(
+                pair[:], window[1, k][:].indirect(offsets[:, PIECE : 2 * PIECE]), u[:], ADD
+            )
+            for r in range(R):
+                latent = zp_sb[:, k, r : r + 1]
+                grown = held.tile([P, E], F32, name=f"grown{k}_{r}")
+                nc.scalar.activation(grown[:], pair[:], EXP, bias=latent)
+                kept = held.tile([P, E], F32, name=f"kept{k}_{r}")
+                nc.vector.tensor_scalar(kept[:], pair[:], latent, 0.0, ADD, MAX)
+                h = held.tile([P, E], BF16, name=f"h{k}_{r}")
+                nc.vector.scalar_tensor_tensor(h[:], grown[:], -1.0, kept[:], ADD, MIN)
+                for m in range(BLOCKS):
+                    nc.tensor.matmul(
+                        acc[m, r][:],
+                        w1_sb[:, k, m * P : (m + 1) * P],
+                        h[:],
+                        start=(k == 0),
+                        stop=(k == BLOCKS - 1),
+                    )
+
+        for r in range(R):
+            for m in range(BLOCKS):
+                bias = b1_sb[:, m : m + 1]
+                grown = held.tile([P, E], F32, name=f"grown_out{m}_{r}")
+                nc.scalar.activation(grown[:], acc[m, r][:], EXP, bias=bias)
+                below = held.tile([P, E], F32, name=f"below{m}_{r}")
+                nc.vector.tensor_scalar(below[:], grown[:], -1.0, 0.0, ADD, MIN)
+                result = held.tile([P, E], F32, name=f"result{m}_{r}")
+                nc.vector.scalar_tensor_tensor(result[:], acc[m, r][:], bias, below[:], ADD, MAX)
+                nc.sync.dma_start(out[m * P : (m + 1) * P, r * E : (r + 1) * E], result[:])

@@ -9,6 +9,7 @@ ADD = mybir.AluOpType.add
 MIN = mybir.AluOpType.min
 MAX = mybir.AluOpType.max
 EXP = mybir.ActivationFunctionType.Exp
+RELU = mybir.ActivationFunctionType.Relu
 
 P = 128
 C = 256
@@ -36,15 +37,15 @@ def tile_bondgraphnetdecoder_kernel(tc, x, b0, zp, w1, b1, offs, out):
                 window[place, k] = held.tile([P, S], F32, name=f"window{place}_{k}")
                 nc.sync.dma_start(window[place, k][:], x[place, k * P : (k + 1) * P, :])
 
+        w1_sb = held.tile([P, BLOCKS, C], BF16, name="w1_sb")
         b0_sb = held.tile([P, BLOCKS], F32, name="b0_sb")
         zp_sb = held.tile([P, BLOCKS, R], F32, name="zp_sb")
         b1_sb = held.tile([P, BLOCKS], F32, name="b1_sb")
-        w1_sb = held.tile([P, BLOCKS, C], BF16, name="w1_sb")
+        nc.scalar.dma_start(w1_sb[:], w1.rearrange("(k p) m -> p k m", p=P))
         with nc.allow_non_contiguous_dma(reason="one to four floats per partition"):
             nc.scalar.dma_start(b0_sb[:], b0.rearrange("(k p) o -> p (k o)", p=P))
             nc.scalar.dma_start(zp_sb[:], zp.rearrange("(k p) r -> p k r", p=P))
             nc.scalar.dma_start(b1_sb[:], b1.rearrange("(k p) o -> p (k o)", p=P))
-        nc.scalar.dma_start(w1_sb[:], w1.rearrange("(k p) m -> p k m", p=P))
 
         zeros = held.tile([P, E], F32, name="zeros")
         nc.vector.memset(zeros[:], 0.0)
@@ -71,26 +72,30 @@ def tile_bondgraphnetdecoder_kernel(tc, x, b0, zp, w1, b1, offs, out):
                 latent = zp_sb[:, k, r : r + 1]
                 grown = held.tile([P, E], F32, name=f"grown{k}_{r}")
                 nc.scalar.activation(grown[:], pair[:], EXP, bias=latent)
-                kept = held.tile([P, E], F32, name=f"kept{k}_{r}")
-                nc.vector.tensor_scalar(kept[:], pair[:], latent, 0.0, ADD, MAX)
-                h = held.tile([P, E], BF16, name=f"h{k}_{r}")
-                nc.vector.scalar_tensor_tensor(h[:], grown[:], -1.0, kept[:], ADD, MIN)
-                for m in range(BLOCKS):
-                    nc.tensor.matmul(
-                        acc[m, r][:],
-                        w1_sb[:, k, m * P : (m + 1) * P],
-                        h[:],
-                        start=(k == 0),
-                        stop=(k == BLOCKS - 1),
-                    )
+                above = held.tile([P, E], BF16, name=f"above{k}_{r}")
+                if k == 0:
+                    nc.scalar.activation(above[:], pair[:], RELU, bias=latent)
+                else:
+                    nc.vector.tensor_scalar(above[:], pair[:], latent, 0.0, ADD, MAX)
+                below = held.tile([P, E], BF16, name=f"below{k}_{r}")
+                nc.vector.tensor_scalar(below[:], grown[:], 1.0, -1.0, MIN, ADD)
+                for half, part in enumerate((above, below)):
+                    for m in range(BLOCKS):
+                        nc.tensor.matmul(
+                            acc[m, r][:],
+                            w1_sb[:, k, m * P : (m + 1) * P],
+                            part[:],
+                            start=(k == 0 and half == 0),
+                            stop=(k == BLOCKS - 1 and half == 1),
+                        )
 
         for r in range(R):
             for m in range(BLOCKS):
                 bias = b1_sb[:, m : m + 1]
                 grown = held.tile([P, E], F32, name=f"grown_out{m}_{r}")
                 nc.scalar.activation(grown[:], acc[m, r][:], EXP, bias=bias)
-                below = held.tile([P, E], F32, name=f"below{m}_{r}")
-                nc.vector.tensor_scalar(below[:], grown[:], -1.0, 0.0, ADD, MIN)
+                capped = held.tile([P, E], F32, name=f"capped{m}_{r}")
+                nc.vector.tensor_scalar(capped[:], grown[:], -1.0, 0.0, ADD, MIN)
                 result = held.tile([P, E], F32, name=f"result{m}_{r}")
-                nc.vector.scalar_tensor_tensor(result[:], acc[m, r][:], bias, below[:], ADD, MAX)
+                nc.vector.scalar_tensor_tensor(result[:], acc[m, r][:], bias, capped[:], ADD, MAX)
                 nc.sync.dma_start(out[m * P : (m + 1) * P, r * E : (r + 1) * E], result[:])

@@ -9,7 +9,6 @@ ADD = mybir.AluOpType.add
 MIN = mybir.AluOpType.min
 MAX = mybir.AluOpType.max
 EXP = mybir.ActivationFunctionType.Exp
-RELU = mybir.ActivationFunctionType.Relu
 
 P = 128
 C = 256
@@ -31,6 +30,11 @@ def tile_bondgraphnetdecoder_kernel(tc, x, b0, zp, w1, b1, offs, out):
 
         offsets = held.tile([P, N // 16], U16, name="offsets")
         nc.sync.dma_start(offsets[:], offs)
+        b0_sb = held.tile([P, BLOCKS], F32, name="b0_sb")
+        zp_sb = held.tile([P, BLOCKS, R], F32, name="zp_sb")
+        with nc.allow_non_contiguous_dma(reason="one to four floats per partition"):
+            nc.sync.dma_start(b0_sb[:], b0.rearrange("(k p) o -> p (k o)", p=P))
+            nc.sync.dma_start(zp_sb[:], zp.rearrange("(k p) r -> p k r", p=P))
         window = {}
         for k in range(BLOCKS):
             for place in range(2):
@@ -38,13 +42,9 @@ def tile_bondgraphnetdecoder_kernel(tc, x, b0, zp, w1, b1, offs, out):
                 nc.sync.dma_start(window[place, k][:], x[place, k * P : (k + 1) * P, :])
 
         w1_sb = held.tile([P, BLOCKS, C], BF16, name="w1_sb")
-        b0_sb = held.tile([P, BLOCKS], F32, name="b0_sb")
-        zp_sb = held.tile([P, BLOCKS, R], F32, name="zp_sb")
         b1_sb = held.tile([P, BLOCKS], F32, name="b1_sb")
         nc.scalar.dma_start(w1_sb[:], w1.rearrange("(k p) m -> p k m", p=P))
-        with nc.allow_non_contiguous_dma(reason="one to four floats per partition"):
-            nc.scalar.dma_start(b0_sb[:], b0.rearrange("(k p) o -> p (k o)", p=P))
-            nc.scalar.dma_start(zp_sb[:], zp.rearrange("(k p) r -> p k r", p=P))
+        with nc.allow_non_contiguous_dma(reason="one float per partition"):
             nc.scalar.dma_start(b1_sb[:], b1.rearrange("(k p) o -> p (k o)", p=P))
 
         zeros = held.tile([P, E], F32, name="zeros")
@@ -73,10 +73,7 @@ def tile_bondgraphnetdecoder_kernel(tc, x, b0, zp, w1, b1, offs, out):
                 grown = held.tile([P, E], F32, name=f"grown{k}_{r}")
                 nc.scalar.activation(grown[:], pair[:], EXP, bias=latent)
                 above = held.tile([P, E], BF16, name=f"above{k}_{r}")
-                if k == 0:
-                    nc.scalar.activation(above[:], pair[:], RELU, bias=latent)
-                else:
-                    nc.vector.tensor_scalar(above[:], pair[:], latent, 0.0, ADD, MAX)
+                nc.vector.tensor_scalar(above[:], pair[:], latent, 0.0, ADD, MAX)
                 below = held.tile([P, E], BF16, name=f"below{k}_{r}")
                 nc.vector.tensor_scalar(below[:], grown[:], 1.0, -1.0, MIN, ADD)
                 for half, part in enumerate((above, below)):

@@ -9,6 +9,7 @@ ADD = mybir.AluOpType.add
 MIN = mybir.AluOpType.min
 MAX = mybir.AluOpType.max
 EXP = mybir.ActivationFunctionType.Exp
+RELU = mybir.ActivationFunctionType.Relu
 
 P = 128
 C = 256
@@ -72,18 +73,26 @@ def tile_bondgraphnetdecoder_kernel(tc, x, b0, zp, w1, b1, offs, out):
                 latent = zp_sb[:, k, r : r + 1]
                 grown = held.tile([P, E], F32, name=f"grown{k}_{r}")
                 nc.scalar.activation(grown[:], pair[:], EXP, bias=latent)
-                above = held.tile([P, E], BF16, name=f"above{k}_{r}")
-                nc.vector.tensor_scalar(above[:], pair[:], latent, 0.0, ADD, MAX)
-                below = held.tile([P, E], BF16, name=f"below{k}_{r}")
-                nc.vector.tensor_scalar(below[:], grown[:], 1.0, -1.0, MIN, ADD)
-                for half, part in enumerate((above, below)):
+                if k == 0 and r % 2 == 1:
+                    ramp = held.tile([P, E], F32, name=f"ramp{r}")
+                    nc.scalar.activation(ramp[:], pair[:], RELU, bias=latent)
+                    whole = held.tile([P, E], BF16, name=f"whole{r}")
+                    nc.vector.scalar_tensor_tensor(whole[:], grown[:], -1.0, ramp[:], ADD, MIN)
+                    parts = (whole,)
+                else:
+                    above = held.tile([P, E], BF16, name=f"above{k}_{r}")
+                    nc.vector.tensor_scalar(above[:], pair[:], latent, 0.0, ADD, MAX)
+                    below = held.tile([P, E], BF16, name=f"below{k}_{r}")
+                    nc.vector.tensor_scalar(below[:], grown[:], 1.0, -1.0, MIN, ADD)
+                    parts = (above, below)
+                for number, part in enumerate(parts):
                     for m in range(BLOCKS):
                         nc.tensor.matmul(
                             acc[m, r][:],
                             w1_sb[:, k, m * P : (m + 1) * P],
                             part[:],
-                            start=(k == 0 and half == 0),
-                            stop=(k == BLOCKS - 1 and half == 1),
+                            start=(k == 0 and number == 0),
+                            stop=(k == BLOCKS - 1 and number == len(parts) - 1),
                         )
 
         for r in range(R):

@@ -100,8 +100,15 @@ def tile_bondgraphnetdecoder_kernel(tc, x, b0, zp, w1, b1, offs, out):
                 bias = b1_sb[:, m : m + 1]
                 grown = held.tile([P, E], F32, name=f"grown_out{m}_{r}")
                 nc.scalar.activation(grown[:], acc[m, r][:], EXP, bias=bias)
-                capped = held.tile([P, E], F32, name=f"capped{m}_{r}")
-                nc.vector.tensor_scalar(capped[:], grown[:], -1.0, 0.0, ADD, MIN)
                 result = held.tile([P, E], F32, name=f"result{m}_{r}")
-                nc.vector.scalar_tensor_tensor(result[:], acc[m, r][:], bias, capped[:], ADD, MAX)
+                if r == R - 1:
+                    ramp = held.tile([P, E], F32, name=f"ramp_out{m}")
+                    nc.scalar.activation(ramp[:], acc[m, r][:], RELU, bias=bias)
+                    nc.vector.scalar_tensor_tensor(result[:], grown[:], -1.0, ramp[:], ADD, MIN)
+                else:
+                    capped = held.tile([P, E], F32, name=f"capped{m}_{r}")
+                    nc.vector.tensor_scalar(capped[:], grown[:], -1.0, 0.0, ADD, MIN)
+                    nc.vector.scalar_tensor_tensor(
+                        result[:], acc[m, r][:], bias, capped[:], ADD, MAX
+                    )
                 nc.sync.dma_start(out[m * P : (m + 1) * P, r * E : (r + 1) * E], result[:])

@@ -19,6 +19,7 @@ R = 4
 N = 2 * E
 BLOCKS = C // P
 PIECE = E // 16
+RAMPED = 3
 
 FLOPS = 2 * C * C * R * E
 
@@ -101,8 +102,8 @@ def tile_bondgraphnetdecoder_kernel(tc, x, b0, zp, w1, b1, offs, out):
                 grown = held.tile([P, E], F32, name=f"grown_out{m}_{r}")
                 nc.scalar.activation(grown[:], acc[m, r][:], EXP, bias=bias)
                 result = held.tile([P, E], F32, name=f"result{m}_{r}")
-                if r == R - 1:
-                    ramp = held.tile([P, E], F32, name=f"ramp_out{m}")
+                if r * BLOCKS + m >= R * BLOCKS - RAMPED:
+                    ramp = held.tile([P, E], F32, name=f"ramp_out{m}_{r}")
                     nc.scalar.activation(ramp[:], acc[m, r][:], RELU, bias=bias)
                     nc.vector.scalar_tensor_tensor(result[:], grown[:], -1.0, ramp[:], ADD, MIN)
                 else:

@@ -32,22 +32,23 @@ def tile_bondgraphnetdecoder_kernel(tc, x, b0, zp, w1, b1, offs, out):
 
         offsets = held.tile([P, N // 16], U16, name="offsets")
         nc.sync.dma_start(offsets[:], offs)
-        b0_sb = held.tile([P, BLOCKS], F32, name="b0_sb")
-        zp_sb = held.tile([P, BLOCKS, R], F32, name="zp_sb")
-        with nc.allow_non_contiguous_dma(reason="one to four floats per partition"):
-            nc.sync.dma_start(b0_sb[:], b0.rearrange("(k p) o -> p (k o)", p=P))
-            nc.sync.dma_start(zp_sb[:], zp.rearrange("(k p) r -> p k r", p=P))
         window = {}
         for k in range(BLOCKS):
             for place in range(2):
                 window[place, k] = held.tile([P, S], F32, name=f"window{place}_{k}")
-                nc.sync.dma_start(window[place, k][:], x[place, k * P : (k + 1) * P, :])
-
-        w1_sb = held.tile([P, BLOCKS, C], BF16, name="w1_sb")
+                nc.sync.dma_start(
+                    window[place, k][:], x[place].rearrange("(p k) s -> p k s", k=BLOCKS)[:, k, :]
+                )
         b1_sb = held.tile([P, BLOCKS], F32, name="b1_sb")
-        nc.scalar.dma_start(w1_sb[:], w1.rearrange("(k p) m -> p k m", p=P))
         with nc.allow_non_contiguous_dma(reason="one float per partition"):
-            nc.scalar.dma_start(b1_sb[:], b1.rearrange("(k p) o -> p (k o)", p=P))
+            nc.sync.dma_start(b1_sb[:], b1.rearrange("(b p) o -> p (b o)", p=P))
+
+        b0_sb = held.tile([P, BLOCKS], F32, name="b0_sb")
+        nc.scalar.dma_start(b0_sb[:], b0.rearrange("(p k) o -> p (k o)", k=BLOCKS))
+        zp_sb = held.tile([P, BLOCKS, R], F32, name="zp_sb")
+        nc.scalar.dma_start(zp_sb[:], zp.rearrange("(p k) r -> p k r", k=BLOCKS))
+        w1_sb = held.tile([P, BLOCKS, C], BF16, name="w1_sb")
+        nc.scalar.dma_start(w1_sb[:], w1.rearrange("(p k) m -> p k m", k=BLOCKS))
 
         zeros = held.tile([P, E], F32, name="zeros")
         nc.vector.memset(zeros[:], 0.0)

@@ -33,12 +33,17 @@ def tile_bondgraphnetdecoder_kernel(tc, x, b0, zp, w1, b1, offs, out):
         offsets = held.tile([P, N // 16], U16, name="offsets")
         nc.sync.dma_start(offsets[:], offs)
         window = {}
+        weights = {}
         for k in range(BLOCKS):
             for place in range(2):
                 window[place, k] = held.tile([P, S], F32, name=f"window{place}_{k}")
                 nc.sync.dma_start(
                     window[place, k][:], x[place].rearrange("(p k) s -> p k s", k=BLOCKS)[:, k, :]
                 )
+            weights[k] = held.tile([P, C], BF16, name=f"weights{k}")
+            nc.sync.dma_start(
+                weights[k][:], w1.rearrange("(p k) m -> p k m", k=BLOCKS)[:, k, :]
+            )
         b1_sb = held.tile([P, BLOCKS], F32, name="b1_sb")
         with nc.allow_non_contiguous_dma(reason="one float per partition"):
             nc.sync.dma_start(b1_sb[:], b1.rearrange("(b p) o -> p (b o)", p=P))
@@ -47,8 +52,6 @@ def tile_bondgraphnetdecoder_kernel(tc, x, b0, zp, w1, b1, offs, out):
         nc.scalar.dma_start(b0_sb[:], b0.rearrange("(p k) o -> p (k o)", k=BLOCKS))
         zp_sb = held.tile([P, BLOCKS, R], F32, name="zp_sb")
         nc.scalar.dma_start(zp_sb[:], zp.rearrange("(p k) r -> p k r", k=BLOCKS))
-        w1_sb = held.tile([P, BLOCKS, C], BF16, name="w1_sb")
-        nc.scalar.dma_start(w1_sb[:], w1.rearrange("(p k) m -> p k m", k=BLOCKS))
 
         zeros = held.tile([P, E], F32, name="zeros")
         nc.vector.memset(zeros[:], 0.0)
@@ -91,7 +94,7 @@ def tile_bondgraphnetdecoder_kernel(tc, x, b0, zp, w1, b1, offs, out):
                     for m in range(BLOCKS):
                         nc.tensor.matmul(
                             acc[m, r][:],
-                            w1_sb[:, k, m * P : (m + 1) * P],
+                            weights[k][:, m * P : (m + 1) * P],
                             part[:],
                             start=(k == 0 and number == 0),
                             stop=(k == BLOCKS - 1 and number == len(parts) - 1),
@@ -106,11 +109,20 @@ def tile_bondgraphnetdecoder_kernel(tc, x, b0, zp, w1, b1, offs, out):
                 if r * BLOCKS + m >= R * BLOCKS - RAMPED:
                     ramp = held.tile([P, E], F32, name=f"ramp_out{m}_{r}")
                     nc.scalar.activation(ramp[:], acc[m, r][:], RELU, bias=bias)
-                    nc.vector.scalar_tensor_tensor(result[:], grown[:], -1.0, ramp[:], ADD, MIN)
+                    halves = 2 if (m, r) == (BLOCKS - 1, R - 1) else 1
+                    for i in range(halves):
+                        half = slice(i * E // halves, (i + 1) * E // halves)
+                        nc.vector.scalar_tensor_tensor(
+                            result[:, half], grown[:, half], -1.0, ramp[:, half], ADD, MIN
+                        )
+                        nc.sync.dma_start(
+                            out[m * P : (m + 1) * P, r * E + half.start : r * E + half.stop],
+                            result[:, half],
+                        )
                 else:
                     capped = held.tile([P, E], F32, name=f"capped{m}_{r}")
                     nc.vector.tensor_scalar(capped[:], grown[:], -1.0, 0.0, ADD, MIN)
                     nc.vector.scalar_tensor_tensor(
                         result[:], acc[m, r][:], bias, capped[:], ADD, MAX
                     )
-                nc.sync.dma_start(out[m * P : (m + 1) * P, r * E : (r + 1) * E], result[:])
+                    nc.sync.dma_start(out[m * P : (m + 1) * P, r * E : (r + 1) * E], result[:])

from contextlib import ExitStack

import concourse.mybir as mybir

F32 = mybir.dt.float32
BF16 = mybir.dt.bfloat16
U16 = mybir.dt.uint16
ADD = mybir.AluOpType.add
MIN = mybir.AluOpType.min
MAX = mybir.AluOpType.max
EXP = mybir.ActivationFunctionType.Exp
RELU = mybir.ActivationFunctionType.Relu

P = 128
C = 256
S = 2048
E = 512
R = 4
N = 2 * E
BLOCKS = C // P
PIECE = E // 16
RAMPED = 3

FLOPS = 2 * C * C * R * E


def tile_bondgraphnetdecoder_kernel(tc, x, b0, zp, w1, b1, offs, out):
    nc = tc.nc
    with ExitStack() as ctx:
        held = ctx.enter_context(tc.tile_pool(name="held", bufs=1))
        psum = ctx.enter_context(tc.psum_pool(name="psum", bufs=1))

        offsets = held.tile([P, N // 16], U16, name="offsets")
        nc.sync.dma_start(offsets[:], offs)
        window = {}
        weights = {}
        for k in range(BLOCKS):
            for place in range(2):
                window[place, k] = held.tile([P, S], F32, name=f"window{place}_{k}")
                nc.sync.dma_start(
                    window[place, k][:], x[place].rearrange("(p k) s -> p k s", k=BLOCKS)[:, k, :]
                )
            weights[k] = held.tile([P, C], BF16, name=f"weights{k}")
            nc.sync.dma_start(
                weights[k][:], w1.rearrange("(p k) m -> p k m", k=BLOCKS)[:, k, :]
            )
        b1_sb = held.tile([P, BLOCKS], F32, name="b1_sb")
        with nc.allow_non_contiguous_dma(reason="one float per partition"):
            nc.sync.dma_start(b1_sb[:], b1.rearrange("(b p) o -> p (b o)", p=P))

        b0_sb = held.tile([P, BLOCKS], F32, name="b0_sb")
        nc.scalar.dma_start(b0_sb[:], b0.rearrange("(p k) o -> p (k o)", k=BLOCKS))
        zp_sb = held.tile([P, BLOCKS, R], F32, name="zp_sb")
        nc.scalar.dma_start(zp_sb[:], zp.rearrange("(p k) r -> p k r", k=BLOCKS))

        zeros = held.tile([P, E], F32, name="zeros")
        nc.vector.memset(zeros[:], 0.0)
        b0_wide = {}
        for k in range(BLOCKS):
            b0_wide[k] = held.tile([P, E], F32, name=f"b0_wide{k}")
            nc.vector.tensor_scalar_add(b0_wide[k][:], zeros[:], b0_sb[:, k : k + 1])

        acc = {}
        for m in range(BLOCKS):
            for r in range(R):
                acc[m, r] = psum.tile([P, E], F32, name=f"acc{m}_{r}")

        for k in range(BLOCKS):
            u = held.tile([P, E], F32, name=f"u{k}")
            nc.vector.tensor_tensor(
                u[:], window[0, k][:].indirect(offsets[:, 0:PIECE]), b0_wide[k][:], ADD
            )
            pair = held.tile([P, E], F32, name=f"pair{k}")
            nc.vector.tensor_tensor(
                pair[:], window[1, k][:].indirect(offsets[:, PIECE : 2 * PIECE]), u[:], ADD
            )
            for r in range(R):
                latent = zp_sb[:, k, r : r + 1]
                grown = held.tile([P, E], F32, name=f"grown{k}_{r}")
                nc.scalar.activation(grown[:], pair[:], EXP, bias=latent)
                if k == 0 and r % 2 == 1:
                    ramp = held.tile([P, E], F32, name=f"ramp{r}")
                    nc.scalar.activation(ramp[:], pair[:], RELU, bias=latent)
                    whole = held.tile([P, E], BF16, name=f"whole{r}")
                    nc.vector.scalar_tensor_tensor(whole[:], grown[:], -1.0, ramp[:], ADD, MIN)
                    parts = (whole,)
                else:
                    above = held.tile([P, E], BF16, name=f"above{k}_{r}")
                    nc.vector.tensor_scalar(above[:], pair[:], latent, 0.0, ADD, MAX)
                    below = held.tile([P, E], BF16, name=f"below{k}_{r}")
                    nc.vector.tensor_scalar(below[:], grown[:], 1.0, -1.0, MIN, ADD)
                    parts = (above, below)
                for number, part in enumerate(parts):
                    for m in range(BLOCKS):
                        nc.tensor.matmul(
                            acc[m, r][:],
                            weights[k][:, m * P : (m + 1) * P],
                            part[:],
                            start=(k == 0 and number == 0),
                            stop=(k == BLOCKS - 1 and number == len(parts) - 1),
                        )

        for r in range(R):
            for m in range(BLOCKS):
                bias = b1_sb[:, m : m + 1]
                grown = held.tile([P, E], F32, name=f"grown_out{m}_{r}")
                nc.scalar.activation(grown[:], acc[m, r][:], EXP, bias=bias)
                result = held.tile([P, E], F32, name=f"result{m}_{r}")
                if r * BLOCKS + m >= R * BLOCKS - RAMPED:
                    ramp = held.tile([P, E], F32, name=f"ramp_out{m}_{r}")
                    nc.scalar.activation(ramp[:], acc[m, r][:], RELU, bias=bias)
                    halves = 2 if (m, r) == (BLOCKS - 1, R - 1) else 1
                    for i in range(halves):
                        half = slice(i * E // halves, (i + 1) * E // halves)
                        nc.vector.scalar_tensor_tensor(
                            result[:, half], grown[:, half], -1.0, ramp[:, half], ADD, MIN
                        )
                        nc.sync.dma_start(
                            out[m * P : (m + 1) * P, r * E + half.start : r * E + half.stop],
                            result[:, half],
                        )
                else:
                    capped = held.tile([P, E], F32, name=f"capped{m}_{r}")
                    nc.vector.tensor_scalar(capped[:], grown[:], -1.0, 0.0, ADD, MIN)
                    nc.vector.scalar_tensor_tensor(
                        result[:], acc[m, r][:], bias, capped[:], ADD, MAX
                    )
                    nc.sync.dma_start(out[m * P : (m + 1) * P, r * E : (r + 1) * E], result[:])
